import numpy as np
import ml_dtypes


def mxq(x, axis, fmt="e4m3"):
    dtype, down = {"e4m3": (ml_dtypes.float8_e4m3fn, 7), "e5m2": (ml_dtypes.float8_e5m2, 14)}[fmt]
    v = np.moveaxis(np.asarray(x, np.float32).astype(ml_dtypes.bfloat16).astype(np.float64), axis, -1)
    blocks = v.reshape(v.shape[:-1] + (-1, 32))
    amax = np.abs(blocks).max(-1, keepdims=True)
    byte = np.maximum(np.where(amax > 0, np.frexp(amax)[1] - 1 + 127, 0) - down, 1)
    scale = np.exp2(byte - 127.0)
    codes = (blocks / scale).astype(np.float32).astype(dtype).astype(np.float64)
    return np.moveaxis((codes * scale).reshape(v.shape), -1, axis)


WIDE = False


def mx_kscale(k):
    if not WIDE:
        return np.ones(k)
    levels = np.array([10, -10, 5, -5, 0])
    a = np.random.permutation(np.resize(levels, k // 512 * 4)).reshape(k // 512, 4)
    idx = np.arange(k)
    return np.exp2(a[idx // 512, idx % 128 // 32])


BF16 = ml_dtypes.bfloat16


def bf(x):
    return np.asarray(x, np.float32).astype(BF16)


def f64(x):
    return np.asarray(x).astype(np.float64)


B, S, E, H, W = 32, 32, 512, 8, 16


def setup_inputs():
    s = mx_kscale(E)
    t = mx_kscale(2 * E)
    th, tv = t[:E], t[E:]
    return {
        "h_ctx": bf(np.random.standard_normal((B, S, E)) * 0.35 * s),
        "v_ctx": bf(np.random.standard_normal((B, S, E)) * 0.35 * s),
        "h_out_w": bf(np.random.standard_normal((E, E)) * 2.5 / np.sqrt(E) / s[None, :] * th[:, None]),
        "h_out_b": bf(np.random.standard_normal(E) * 0.2 * th),
        "v_out_w": bf(np.random.standard_normal((E, E)) * 2.5 / np.sqrt(E) / s[None, :] * tv[:, None]),
        "v_out_b": bf(np.random.standard_normal(E) * 0.2 * tv),
        "mlp_w1": bf(np.random.standard_normal((E, 2 * E)) / np.sqrt(2 * E) / t[None, :]),
        "mlp_b1": bf(np.random.standard_normal(E) * 0.2),
    }


def reference(h_ctx, v_ctx, h_out_w, h_out_b, v_out_w, v_out_b, mlp_w1, mlp_b1):
    h_out = (mxq(f64(h_ctx), 2, "e4m3") @ mxq(f64(h_out_w), 1, "e4m3").T) + f64(h_out_b)
    v_out = (mxq(f64(v_ctx), 2, "e4m3") @ mxq(f64(v_out_w), 1, "e4m3").T) + f64(v_out_b)
    combined = np.concatenate([h_out, v_out], axis=-1)
    return np.maximum((mxq(combined, 2, "e4m3") @ mxq(f64(mlp_w1), 1, "e4m3").T) + f64(mlp_b1), 0.0)

@@ -1,0 +1,214 @@
+from contextlib import ExitStack
+
+import concourse.mybir as mybir
+from concourse.masks import make_identity
+
+F32 = mybir.dt.float32
+BF16 = mybir.dt.bfloat16
+U32 = mybir.dt.uint32
+U8 = mybir.dt.uint8
+FP8X4 = mybir.dt.float8_e4m3fn_x4
+ADD = mybir.AluOpType.add
+IDENTITY = mybir.ActivationFunctionType.Identity
+RELU = mybir.ActivationFunctionType.Relu
+
+P = 128
+PACK = 4
+K_PASS = P * PACK
+PASS_WORDS = K_PASS // 2
+HALVES = 2
+E = 512
+TOKENS = 1024
+TOKEN_TILES = TOKENS // P
+BRANCHES = 2
+CHUNKS = E // P
+PAIR = 2
+PAIR_COLS = PAIR * P
+BLOCK = PAIR_COLS
+BLOCKS = TOKENS // BLOCK
+BANKS = 8
+
+FLOPS = 2 * TOKENS * E * E * BRANCHES + 2 * TOKENS * (BRANCHES * E) * E
+
+
+def tile_bispa_pa_kernel(
+    tc, h_ctx, v_ctx, h_out_w, h_out_b, v_out_w, v_out_b, mlp_w1, mlp_b1, out
+):
+    nc = tc.nc
+    with ExitStack() as stack:
+        stack.enter_context(tc.manual_schedule())
+        keep = stack.enter_context(tc.tile_pool(name="keep", bufs=1))
+        stage = stack.enter_context(tc.tile_pool(name="stage", bufs=4))
+        psum = stack.enter_context(tc.psum_pool(name="psum", bufs=BANKS))
+
+        ctx_rows = [
+            ctx.flatten_outer_dims().rearrange("(p i) k -> p i k", i=TOKEN_TILES) for ctx in (h_ctx, v_ctx)
+        ]
+        out_rows = out.flatten_outer_dims().rearrange("(p i) f -> p i f", i=TOKEN_TILES)
+        proj_rows = [w.rearrange("(u p e) k -> p u e k", u=HALVES, e=2) for w in (h_out_w, v_out_w)]
+        proj_bias_rows = [b.rearrange("(u p e) -> p u e", u=HALVES, e=2) for b in (h_out_b, v_out_b)]
+        mlp_rows = mlp_w1.rearrange("(j p) k -> p j k", p=P)
+
+        ctx_sb = keep.tile([P, BRANCHES, TOKEN_TILES, E], BF16)
+        proj_sb = keep.tile([P, BRANCHES, HALVES, 2, E], BF16)
+        mlp_sb = keep.tile([P, CHUNKS, BRANCHES * E], BF16)
+        proj_bias_bf = [keep.tile([P, HALVES, 2], BF16, name="proj_bias_bf%d" % g) for g in range(BRANCHES)]
+        bias_row = keep.tile([P, E], BF16)
+        nc.vector.memset(bias_row[:], 0.0)
+
+        def load_projection(g):
+            for u in range(HALVES):
+                nc.sync.dma_start(out=proj_sb[:, g, u], in_=proj_rows[g][:, u])
+
+        def load_context(g, b):
+            tiles = slice(b * PAIR, (b + 1) * PAIR)
+            nc.sync.dma_start(out=ctx_sb[:, g, tiles], in_=ctx_rows[g][:, tiles])
+
+        load_projection(0)
+        load_context(0, 0)
+        for g in range(BRANCHES):
+            nc.sync.dma_start(out=proj_bias_bf[g][:], in_=proj_bias_rows[g])
+        nc.sync.dma_start(out=bias_row[0:1, :], in_=mlp_b1.rearrange("(o f) -> o f", o=1))
+        load_projection(1)
+        load_context(1, 0)
+        for b in range(1, BLOCKS):
+            for g in range(BRANCHES):
+                load_context(g, b)
+        for j in range(0, CHUNKS, PAIR):
+            nc.sync.dma_start(out=mlp_sb[:, j : j + PAIR], in_=mlp_rows[:, j : j + PAIR])
+
+        ident = keep.tile([P, P], F32)
+        make_identity(nc, ident[:])
+        ones = keep.tile([P, P], BF16)
+        nc.vector.memset(ones[:], 1.0)
+
+        ctx_q = keep.tile([P, BRANCHES, TOKENS], U32, align_bytes=64)
+        ctx_s = keep.tile([P, BRANCHES, TOKENS], U8, align_bytes=64)
+        proj_q = keep.tile([P, BRANCHES, E], U32, align_bytes=64)
+        proj_s = keep.tile([P, BRANCHES, E], U8, align_bytes=64)
+        mlp_q = keep.tile([P, BRANCHES, E], U32, align_bytes=64)
+        mlp_s = keep.tile([P, BRANCHES, E], U8, align_bytes=64)
+        comb_q = keep.tile([P, BRANCHES, TOKENS], U32, align_bytes=64)
+        comb_s = keep.tile([P, BRANCHES, TOKENS], U8, align_bytes=64)
+
+        def quantise_rows(words, codes, scales, copy):
+            planes = psum.tile([P, PAIR, HALVES, P], F32, tag="bank")
+            for r in range(PAIR):
+                for u in range(HALVES):
+                    nc.tensor.transpose(planes[:, r, u, :], words[:, r, u * P : (u + 1) * P], ident[:])
+            grouped = stage.tile([P, PAIR_COLS, PACK], BF16, align_bytes=64)
+            copy(
+                out=grouped[:].bitcast(F32).rearrange("p (r c) u -> p r c u", r=PAIR),
+                in_=planes[:].rearrange("p r u c -> p r c u"),
+            )
+            nc.vector.quantize_mx(
+                out=codes.bitcast(FP8X4), scales=scales, in_=grouped[:].rearrange("p c t -> p (c t)")
+            )
+
+        ctx_words = ctx_sb[:].bitcast(F32)
+        proj_words = proj_sb[:].bitcast(F32)
+        mlp_words = mlp_sb[:].bitcast(F32)
+
+        def quantise_projection(g):
+            for u, copy in enumerate((nc.scalar.copy, nc.vector.tensor_copy)):
+                cols = slice(u * PAIR_COLS, (u + 1) * PAIR_COLS)
+                quantise_rows(proj_words[:, g, u], proj_q[:, g, cols], proj_s[:, g, cols], copy)
+
+        def quantise_context(g, b):
+            cols = slice(b * BLOCK, (b + 1) * BLOCK)
+            quantise_rows(
+                ctx_words[:, g, b * PAIR : (b + 1) * PAIR], ctx_q[:, g, cols], ctx_s[:, g, cols], nc.scalar.copy
+            )
+
+        def quantise_mlp():
+            for j in range(0, CHUNKS, PAIR):
+                cols = slice(j * P, (j + PAIR) * P)
+                for g in range(BRANCHES):
+                    quantise_rows(
+                        mlp_words[:, j : j + PAIR, g * PASS_WORDS : (g + 1) * PASS_WORDS],
+                        mlp_q[:, g, cols],
+                        mlp_s[:, g, cols],
+                        nc.scalar.copy,
+                    )
+
+        proj_bias = keep.tile([P, BRANCHES, CHUNKS], F32)
+        mlp_bias = keep.tile([P, E], F32)
+
+        def prepare_biases():
+            for g in range(BRANCHES):
+                nc.vector.tensor_copy(out=proj_bias[:, g], in_=proj_bias_bf[g][:].rearrange("p u e -> p (u e)"))
+            bias_bank = psum.tile([P, E], F32, tag="bank")
+            nc.tensor.matmul(out=bias_bank[:], lhsT=ones[:], rhs=bias_row[:], start=True, stop=True)
+            nc.vector.tensor_copy(out=mlp_bias[:], in_=bias_bank[:])
+
+        def stage_one(b):
+            tokens = slice(b * BLOCK, (b + 1) * BLOCK)
+            combined = stage.tile([P, BRANCHES, CHUNKS, BLOCK], BF16)
+            for g in range(BRANCHES):
+                for c0 in range(0, CHUNKS, PAIR):
+                    proj = psum.tile([P, PAIR, BLOCK], F32, tag="bank")
+                    for n in range(PAIR):
+                        feats = slice((c0 + n) * P, (c0 + n + 1) * P)
+                        nc.tensor.matmul_mx(
+                            out=proj[:, n, :],
+                            lhsT=proj_q[:, g, feats].bitcast(FP8X4),
+                            lhsT_scale=proj_s[:, g, feats],
+                            rhs=ctx_q[:, g, tokens].bitcast(FP8X4),
+                            rhs_scale=ctx_s[:, g, tokens],
+                            start=True,
+                            stop=True,
+                        )
+                    last_bank = g == BRANCHES - 1 and c0 == CHUNKS - PAIR
+                    for n in range(PAIR):
+                        bias = proj_bias[:, g, c0 + n : c0 + n + 1]
+                        if last_bank:
+                            nc.vector.tensor_scalar_add(out=combined[:, g, c0 + n, :], in0=proj[:, n, :], scalar1=bias)
+                        else:
+                            nc.scalar.activation(
+                                out=combined[:, g, c0 + n, :], in_=proj[:, n, :], func=IDENTITY, bias=bias
+                            )
+            grouped = stage.tile([P, BRANCHES, BLOCK, PACK], BF16, align_bytes=64, name="grouped_combined")
+            for g in range(BRANCHES):
+                nc.vector.tensor_copy(
+                    out=grouped[:, g].rearrange("p (c i) t -> p c t i", i=4),
+                    in_=combined[:, g].rearrange("p t (c i) -> p c t i", i=4),
+                )
+            for g in range(BRANCHES):
+                nc.vector.quantize_mx(
+                    out=comb_q[:, g, tokens].bitcast(FP8X4),
+                    scales=comb_s[:, g, tokens],
+                    in_=grouped[:, g].rearrange("p w t -> p (w t)"),
+                )
+
+        def stage_two(i):
+            toks = slice(i * P, (i + 1) * P)
+            acc = psum.tile([P, E], F32, tag="bank")
+            for g in range(BRANCHES):
+                nc.tensor.matmul_mx(
+                    out=acc[:],
+                    lhsT=comb_q[:, g, toks].bitcast(FP8X4),
+                    lhsT_scale=comb_s[:, g, toks],
+                    rhs=mlp_q[:, g, :].bitcast(FP8X4),
+                    rhs_scale=mlp_s[:, g, :],
+                    start=(g == 0),
+                    stop=(g == BRANCHES - 1),
+                )
+            biased = stage.tile([P, E], F32)
+            nc.vector.tensor_tensor(out=biased[:], in0=acc[:], in1=mlp_bias[:], op=ADD)
+            hidden = stage.tile([P, E], F32)
+            nc.scalar.activation(out=hidden[:], in_=biased[:], func=RELU)
+            nc.sync.dma_start(out=out_rows[:, i, :], in_=hidden[:])
+
+        for g in range(BRANCHES):
+            quantise_projection(g)
+            quantise_context(g, 0)
+        prepare_biases()
+        for b in range(BLOCKS):
+            if b + 1 < BLOCKS:
+                for g in range(BRANCHES):
+                    quantise_context(g, b + 1)
+            else:
+                quantise_mlp()
+            stage_one(b)
+        for i in range(TOKEN_TILES):
+            stage_two(i)

@@ -26,6 +26,8 @@ PAIR = 2
 PAIR_COLS = PAIR * P
 BLOCK = PAIR_COLS
 BLOCKS = TOKENS // BLOCK
+AHEAD = 4
+PER_STEP = 2
 BANKS = 8
 
 FLOPS = 2 * TOKENS * E * E * BRANCHES + 2 * TOKENS * (BRANCHES * E) * E
@@ -39,6 +41,7 @@ def tile_bispa_pa_kernel(
         stack.enter_context(tc.manual_schedule())
         keep = stack.enter_context(tc.tile_pool(name="keep", bufs=1))
         stage = stack.enter_context(tc.tile_pool(name="stage", bufs=4))
+        results = stack.enter_context(tc.tile_pool(name="results", bufs=TOKEN_TILES))
         psum = stack.enter_context(tc.psum_pool(name="psum", bufs=BANKS))
 
         ctx_rows = [
@@ -64,16 +67,14 @@ def tile_bispa_pa_kernel(
             tiles = slice(b * PAIR, (b + 1) * PAIR)
             nc.sync.dma_start(out=ctx_sb[:, g, tiles], in_=ctx_rows[g][:, tiles])
 
-        load_projection(0)
-        load_context(0, 0)
         for g in range(BRANCHES):
-            nc.sync.dma_start(out=proj_bias_bf[g][:], in_=proj_bias_rows[g])
-        nc.sync.dma_start(out=bias_row[0:1, :], in_=mlp_b1.rearrange("(o f) -> o f", o=1))
-        load_projection(1)
-        load_context(1, 0)
-        for b in range(1, BLOCKS):
-            for g in range(BRANCHES):
+            load_projection(g)
+            for b in range(BLOCKS):
                 load_context(g, b)
+                if g == 0 and b == 0:
+                    for branch in range(BRANCHES):
+                        nc.sync.dma_start(out=proj_bias_bf[branch][:], in_=proj_bias_rows[branch])
+                    nc.sync.dma_start(out=bias_row[0:1, :], in_=mlp_b1.rearrange("(o f) -> o f", o=1))
         for j in range(0, CHUNKS, PAIR):
             nc.sync.dma_start(out=mlp_sb[:, j : j + PAIR], in_=mlp_rows[:, j : j + PAIR])
 
@@ -91,13 +92,13 @@ def tile_bispa_pa_kernel(
         comb_q = keep.tile([P, BRANCHES, TOKENS], U32, align_bytes=64)
         comb_s = keep.tile([P, BRANCHES, TOKENS], U8, align_bytes=64)
 
-        def quantise_rows(words, codes, scales, copy):
+        def quantise_rows(words, codes, scales):
             planes = psum.tile([P, PAIR, HALVES, P], F32, tag="bank")
             for r in range(PAIR):
                 for u in range(HALVES):
                     nc.tensor.transpose(planes[:, r, u, :], words[:, r, u * P : (u + 1) * P], ident[:])
             grouped = stage.tile([P, PAIR_COLS, PACK], BF16, align_bytes=64)
-            copy(
+            nc.scalar.copy(
                 out=grouped[:].bitcast(F32).rearrange("p (r c) u -> p r c u", r=PAIR),
                 in_=planes[:].rearrange("p r u c -> p r c u"),
             )
@@ -109,27 +110,19 @@ def tile_bispa_pa_kernel(
         proj_words = proj_sb[:].bitcast(F32)
         mlp_words = mlp_sb[:].bitcast(F32)
 
-        def quantise_projection(g):
-            for u, copy in enumerate((nc.scalar.copy, nc.vector.tensor_copy)):
-                cols = slice(u * PAIR_COLS, (u + 1) * PAIR_COLS)
-                quantise_rows(proj_words[:, g, u], proj_q[:, g, cols], proj_s[:, g, cols], copy)
-
-        def quantise_context(g, b):
-            cols = slice(b * BLOCK, (b + 1) * BLOCK)
-            quantise_rows(
-                ctx_words[:, g, b * PAIR : (b + 1) * PAIR], ctx_q[:, g, cols], ctx_s[:, g, cols], nc.scalar.copy
-            )
-
-        def quantise_mlp():
-            for j in range(0, CHUNKS, PAIR):
-                cols = slice(j * P, (j + PAIR) * P)
-                for g in range(BRANCHES):
-                    quantise_rows(
-                        mlp_words[:, j : j + PAIR, g * PASS_WORDS : (g + 1) * PASS_WORDS],
-                        mlp_q[:, g, cols],
-                        mlp_s[:, g, cols],
-                        nc.scalar.copy,
-                    )
+        pieces = []
+        for g in range(BRANCHES):
+            for n in range(E // PAIR_COLS):
+                cols = slice(n * PAIR_COLS, (n + 1) * PAIR_COLS)
+                pieces.append((proj_words[:, g, n], proj_q[:, g, cols], proj_s[:, g, cols]))
+            for n in range(BLOCKS):
+                cols = slice(n * PAIR_COLS, (n + 1) * PAIR_COLS)
+                pieces.append((ctx_words[:, g, n * PAIR : (n + 1) * PAIR], ctx_q[:, g, cols], ctx_s[:, g, cols]))
+        for n in range(E // PAIR_COLS):
+            cols = slice(n * PAIR_COLS, (n + 1) * PAIR_COLS)
+            for g in range(BRANCHES):
+                words = mlp_words[:, n * PAIR : (n + 1) * PAIR, g * PASS_WORDS : (g + 1) * PASS_WORDS]
+                pieces.append((words, mlp_q[:, g, cols], mlp_s[:, g, cols]))
 
         proj_bias = keep.tile([P, BRANCHES, CHUNKS], F32)
         mlp_bias = keep.tile([P, E], F32)
@@ -141,44 +134,49 @@ def tile_bispa_pa_kernel(
             nc.tensor.matmul(out=bias_bank[:], lhsT=ones[:], rhs=bias_row[:], start=True, stop=True)
             nc.vector.tensor_copy(out=mlp_bias[:], in_=bias_bank[:])
 
-        def stage_one(b):
+        def project(g, i):
+            toks = slice(i * P, (i + 1) * P)
+            proj = psum.tile([P, CHUNKS, P], F32, tag="bank")
+            for t in range(CHUNKS):
+                feats = slice(t * P, (t + 1) * P)
+                nc.tensor.matmul_mx(
+                    out=proj[:, t, :],
+                    lhsT=proj_q[:, g, feats].bitcast(FP8X4),
+                    lhsT_scale=proj_s[:, g, feats],
+                    rhs=ctx_q[:, g, toks].bitcast(FP8X4),
+                    rhs_scale=ctx_s[:, g, toks],
+                    start=True,
+                    stop=True,
+                )
+            return proj
+
+        def stage_one(g, b):
+            first, second = project(g, b * PAIR), project(g, b * PAIR + 1)
+            grouped = stage.tile([P, PAIR, P, PACK], BF16, align_bytes=64, name="grouped_combined")
+            chunks = stage.tile([P, CHUNKS, P], BF16)
+            for t in range(CHUNKS):
+                nc.scalar.activation(
+                    out=chunks[:, t, :], in_=first[:, t, :], func=IDENTITY, bias=proj_bias[:, g, t : t + 1]
+                )
+            nc.vector.tensor_tensor(
+                out=grouped[:, 1],
+                in0=second[:].rearrange("p t w -> p w t"),
+                in1=proj_bias[:, g, :].unsqueeze(1).to_broadcast([P, P, CHUNKS]),
+                op=ADD,
+            )
+            nc.vector.tensor_copy(
+                out=grouped[:, 0].rearrange("p (c i) t -> p c t i", i=4),
+                in_=chunks[:].rearrange("p t (c i) -> p c t i", i=4),
+            )
+            return grouped
+
+        def quantise_combined(g, b, grouped):
             tokens = slice(b * BLOCK, (b + 1) * BLOCK)
-            combined = stage.tile([P, BRANCHES, CHUNKS, BLOCK], BF16)
-            for g in range(BRANCHES):
-                for c0 in range(0, CHUNKS, PAIR):
-                    proj = psum.tile([P, PAIR, BLOCK], F32, tag="bank")
-                    for n in range(PAIR):
-                        feats = slice((c0 + n) * P, (c0 + n + 1) * P)
-                        nc.tensor.matmul_mx(
-                            out=proj[:, n, :],
-                            lhsT=proj_q[:, g, feats].bitcast(FP8X4),
-                            lhsT_scale=proj_s[:, g, feats],
-                            rhs=ctx_q[:, g, tokens].bitcast(FP8X4),
-                            rhs_scale=ctx_s[:, g, tokens],
-                            start=True,
-                            stop=True,
-                        )
-                    last_bank = g == BRANCHES - 1 and c0 == CHUNKS - PAIR
-                    for n in range(PAIR):
-                        bias = proj_bias[:, g, c0 + n : c0 + n + 1]
-                        if last_bank:
-                            nc.vector.tensor_scalar_add(out=combined[:, g, c0 + n, :], in0=proj[:, n, :], scalar1=bias)
-                        else:
-                            nc.scalar.activation(
-                                out=combined[:, g, c0 + n, :], in_=proj[:, n, :], func=IDENTITY, bias=bias
-                            )
-            grouped = stage.tile([P, BRANCHES, BLOCK, PACK], BF16, align_bytes=64, name="grouped_combined")
-            for g in range(BRANCHES):
-                nc.vector.tensor_copy(
-                    out=grouped[:, g].rearrange("p (c i) t -> p c t i", i=4),
-                    in_=combined[:, g].rearrange("p t (c i) -> p c t i", i=4),
-                )
-            for g in range(BRANCHES):
-                nc.vector.quantize_mx(
-                    out=comb_q[:, g, tokens].bitcast(FP8X4),
-                    scales=comb_s[:, g, tokens],
-                    in_=grouped[:, g].rearrange("p w t -> p (w t)"),
-                )
+            nc.vector.quantize_mx(
+                out=comb_q[:, g, tokens].bitcast(FP8X4),
+                scales=comb_s[:, g, tokens],
+                in_=grouped[:].rearrange("p s w t -> p (s w t)"),
+            )
 
         def stage_two(i):
             toks = slice(i * P, (i + 1) * P)
@@ -193,22 +191,23 @@ def tile_bispa_pa_kernel(
                     start=(g == 0),
                     stop=(g == BRANCHES - 1),
                 )
-            biased = stage.tile([P, E], F32)
+            biased = results.tile([P, E], F32)
             nc.vector.tensor_tensor(out=biased[:], in0=acc[:], in1=mlp_bias[:], op=ADD)
-            hidden = stage.tile([P, E], F32)
+            hidden = results.tile([P, E], F32)
             nc.scalar.activation(out=hidden[:], in_=biased[:], func=RELU)
             nc.sync.dma_start(out=out_rows[:, i, :], in_=hidden[:])
 
-        for g in range(BRANCHES):
-            quantise_projection(g)
-            quantise_context(g, 0)
+        for piece in pieces[:AHEAD]:
+            quantise_rows(piece[0], piece[1], piece[2])
         prepare_biases()
-        for b in range(BLOCKS):
-            if b + 1 < BLOCKS:
-                for g in range(BRANCHES):
-                    quantise_context(g, b + 1)
-            else:
-                quantise_mlp()
-            stage_one(b)
+        step = 0
+        for g in range(BRANCHES):
+            for b in range(BLOCKS):
+                grouped = stage_one(g, b)
+                done = AHEAD + step * PER_STEP
+                for piece in pieces[done : done + PER_STEP]:
+                    quantise_rows(piece[0], piece[1], piece[2])
+                quantise_combined(g, b, grouped)
+                step += 1
         for i in range(TOKEN_TILES):
             stage_two(i)

@@ -28,6 +28,7 @@ BLOCK = PAIR_COLS
 BLOCKS = TOKENS // BLOCK
 AHEAD = 4
 PER_STEP = 2
+WARM_UP = 4
 BANKS = 8
 
 FLOPS = 2 * TOKENS * E * E * BRANCHES + 2 * TOKENS * (BRANCHES * E) * E
@@ -56,6 +57,8 @@ def tile_bispa_pa_kernel(
         proj_sb = keep.tile([P, BRANCHES, HALVES, 2, E], BF16)
         mlp_sb = keep.tile([P, CHUNKS, BRANCHES * E], BF16)
         proj_bias_bf = [keep.tile([P, HALVES, 2], BF16, name="proj_bias_bf%d" % g) for g in range(BRANCHES)]
+        ones = keep.tile([P, E], BF16)
+        nc.vector.memset(ones[:], 1.0)
         bias_row = keep.tile([P, E], BF16)
         nc.vector.memset(bias_row[:], 0.0)
 
@@ -80,8 +83,11 @@ def tile_bispa_pa_kernel(
 
         ident = keep.tile([P, P], F32)
         make_identity(nc, ident[:])
-        ones = keep.tile([P, P], BF16)
-        nc.vector.memset(ones[:], 1.0)
+
+        def idle_matmuls(count):
+            unread = psum.tile([P, E], F32, tag="bank")
+            for n in range(count):
+                nc.tensor.matmul(out=unread[:], lhsT=ones[:, :P], rhs=ones[:], start=True, stop=True)
 
         ctx_q = keep.tile([P, BRANCHES, TOKENS], U32, align_bytes=64)
         ctx_s = keep.tile([P, BRANCHES, TOKENS], U8, align_bytes=64)
@@ -124,15 +130,13 @@ def tile_bispa_pa_kernel(
                 words = mlp_words[:, n * PAIR : (n + 1) * PAIR, g * PASS_WORDS : (g + 1) * PASS_WORDS]
                 pieces.append((words, mlp_q[:, g, cols], mlp_s[:, g, cols]))
 
-        proj_bias = keep.tile([P, BRANCHES, CHUNKS], F32)
+        proj_bias = [bias[:].rearrange("p u e -> p (u e)") for bias in proj_bias_bf]
         mlp_bias = keep.tile([P, E], F32)
 
-        def prepare_biases():
-            for g in range(BRANCHES):
-                nc.vector.tensor_copy(out=proj_bias[:, g], in_=proj_bias_bf[g][:].rearrange("p u e -> p (u e)"))
+        def spread_mlp_bias():
             bias_bank = psum.tile([P, E], F32, tag="bank")
-            nc.tensor.matmul(out=bias_bank[:], lhsT=ones[:], rhs=bias_row[:], start=True, stop=True)
-            nc.vector.tensor_copy(out=mlp_bias[:], in_=bias_bank[:])
+            nc.tensor.matmul(out=bias_bank[:], lhsT=ones[:, :P], rhs=bias_row[:], start=True, stop=True)
+            nc.scalar.copy(out=mlp_bias[:], in_=bias_bank[:])
 
         def project(g, i):
             toks = slice(i * P, (i + 1) * P)
@@ -156,12 +160,12 @@ def tile_bispa_pa_kernel(
             chunks = stage.tile([P, CHUNKS, P], BF16)
             for t in range(CHUNKS):
                 nc.scalar.activation(
-                    out=chunks[:, t, :], in_=first[:, t, :], func=IDENTITY, bias=proj_bias[:, g, t : t + 1]
+                    out=chunks[:, t, :], in_=first[:, t, :], func=IDENTITY, bias=proj_bias[g][:, t : t + 1]
                 )
             nc.vector.tensor_tensor(
                 out=grouped[:, 1],
                 in0=second[:].rearrange("p t w -> p w t"),
-                in1=proj_bias[:, g, :].unsqueeze(1).to_broadcast([P, P, CHUNKS]),
+                in1=proj_bias[g].unsqueeze(1).to_broadcast([P, P, CHUNKS]),
                 op=ADD,
             )
             nc.vector.tensor_copy(
@@ -197,9 +201,10 @@ def tile_bispa_pa_kernel(
             nc.scalar.activation(out=hidden[:], in_=biased[:], func=RELU)
             nc.sync.dma_start(out=out_rows[:, i, :], in_=hidden[:])
 
+        idle_matmuls(WARM_UP)
         for piece in pieces[:AHEAD]:
             quantise_rows(piece[0], piece[1], piece[2])
-        prepare_biases()
+            idle_matmuls(1)
         step = 0
         for g in range(BRANCHES):
             for b in range(BLOCKS):
@@ -209,5 +214,6 @@ def tile_bispa_pa_kernel(
                     quantise_rows(piece[0], piece[1], piece[2])
                 quantise_combined(g, b, grouped)
                 step += 1
+        spread_mlp_bias()
         for i in range(TOKEN_TILES):
             stage_two(i)

@@ -28,7 +28,6 @@ BLOCK = PAIR_COLS
 BLOCKS = TOKENS // BLOCK
 AHEAD = 4
 PER_STEP = 2
-WARM_UP = 4
 BANKS = 8
 
 FLOPS = 2 * TOKENS * E * E * BRANCHES + 2 * TOKENS * (BRANCHES * E) * E
@@ -83,11 +82,6 @@ def tile_bispa_pa_kernel(
 
         ident = keep.tile([P, P], F32)
         make_identity(nc, ident[:])
-
-        def idle_matmuls(count):
-            unread = psum.tile([P, E], F32, tag="bank")
-            for n in range(count):
-                nc.tensor.matmul(out=unread[:], lhsT=ones[:, :P], rhs=ones[:], start=True, stop=True)
 
         ctx_q = keep.tile([P, BRANCHES, TOKENS], U32, align_bytes=64)
         ctx_s = keep.tile([P, BRANCHES, TOKENS], U8, align_bytes=64)
@@ -201,10 +195,8 @@ def tile_bispa_pa_kernel(
             nc.scalar.activation(out=hidden[:], in_=biased[:], func=RELU)
             nc.sync.dma_start(out=out_rows[:, i, :], in_=hidden[:])
 
-        idle_matmuls(WARM_UP)
         for piece in pieces[:AHEAD]:
             quantise_rows(piece[0], piece[1], piece[2])
-            idle_matmuls(1)
         step = 0
         for g in range(BRANCHES):
             for b in range(BLOCKS):

from contextlib import ExitStack

import concourse.mybir as mybir
from concourse.masks import make_identity

F32 = mybir.dt.float32
BF16 = mybir.dt.bfloat16
U32 = mybir.dt.uint32
U8 = mybir.dt.uint8
FP8X4 = mybir.dt.float8_e4m3fn_x4
ADD = mybir.AluOpType.add
IDENTITY = mybir.ActivationFunctionType.Identity
RELU = mybir.ActivationFunctionType.Relu

P = 128
PACK = 4
K_PASS = P * PACK
PASS_WORDS = K_PASS // 2
HALVES = 2
E = 512
TOKENS = 1024
TOKEN_TILES = TOKENS // P
BRANCHES = 2
CHUNKS = E // P
PAIR = 2
PAIR_COLS = PAIR * P
BLOCK = PAIR_COLS
BLOCKS = TOKENS // BLOCK
AHEAD = 4
PER_STEP = 2
BANKS = 8

FLOPS = 2 * TOKENS * E * E * BRANCHES + 2 * TOKENS * (BRANCHES * E) * E


def tile_bispa_pa_kernel(
    tc, h_ctx, v_ctx, h_out_w, h_out_b, v_out_w, v_out_b, mlp_w1, mlp_b1, out
):
    nc = tc.nc
    with ExitStack() as stack:
        stack.enter_context(tc.manual_schedule())
        keep = stack.enter_context(tc.tile_pool(name="keep", bufs=1))
        stage = stack.enter_context(tc.tile_pool(name="stage", bufs=4))
        results = stack.enter_context(tc.tile_pool(name="results", bufs=TOKEN_TILES))
        psum = stack.enter_context(tc.psum_pool(name="psum", bufs=BANKS))

        ctx_rows = [
            ctx.flatten_outer_dims().rearrange("(p i) k -> p i k", i=TOKEN_TILES) for ctx in (h_ctx, v_ctx)
        ]
        out_rows = out.flatten_outer_dims().rearrange("(p i) f -> p i f", i=TOKEN_TILES)
        proj_rows = [w.rearrange("(u p e) k -> p u e k", u=HALVES, e=2) for w in (h_out_w, v_out_w)]
        proj_bias_rows = [b.rearrange("(u p e) -> p u e", u=HALVES, e=2) for b in (h_out_b, v_out_b)]
        mlp_rows = mlp_w1.rearrange("(j p) k -> p j k", p=P)

        ctx_sb = keep.tile([P, BRANCHES, TOKEN_TILES, E], BF16)
        proj_sb = keep.tile([P, BRANCHES, HALVES, 2, E], BF16)
        mlp_sb = keep.tile([P, CHUNKS, BRANCHES * E], BF16)
        proj_bias_bf = [keep.tile([P, HALVES, 2], BF16, name="proj_bias_bf%d" % g) for g in range(BRANCHES)]
        ones = keep.tile([P, E], BF16)
        nc.vector.memset(ones[:], 1.0)
        bias_row = keep.tile([P, E], BF16)
        nc.vector.memset(bias_row[:], 0.0)

        def load_projection(g):
            for u in range(HALVES):
                nc.sync.dma_start(out=proj_sb[:, g, u], in_=proj_rows[g][:, u])

        def load_context(g, b):
            tiles = slice(b * PAIR, (b + 1) * PAIR)
            nc.sync.dma_start(out=ctx_sb[:, g, tiles], in_=ctx_rows[g][:, tiles])

        for g in range(BRANCHES):
            load_projection(g)
            for b in range(BLOCKS):
                load_context(g, b)
                if g == 0 and b == 0:
                    for branch in range(BRANCHES):
                        nc.sync.dma_start(out=proj_bias_bf[branch][:], in_=proj_bias_rows[branch])
                    nc.sync.dma_start(out=bias_row[0:1, :], in_=mlp_b1.rearrange("(o f) -> o f", o=1))
        for j in range(0, CHUNKS, PAIR):
            nc.sync.dma_start(out=mlp_sb[:, j : j + PAIR], in_=mlp_rows[:, j : j + PAIR])

        ident = keep.tile([P, P], F32)
        make_identity(nc, ident[:])

        ctx_q = keep.tile([P, BRANCHES, TOKENS], U32, align_bytes=64)
        ctx_s = keep.tile([P, BRANCHES, TOKENS], U8, align_bytes=64)
        proj_q = keep.tile([P, BRANCHES, E], U32, align_bytes=64)
        proj_s = keep.tile([P, BRANCHES, E], U8, align_bytes=64)
        mlp_q = keep.tile([P, BRANCHES, E], U32, align_bytes=64)
        mlp_s = keep.tile([P, BRANCHES, E], U8, align_bytes=64)
        comb_q = keep.tile([P, BRANCHES, TOKENS], U32, align_bytes=64)
        comb_s = keep.tile([P, BRANCHES, TOKENS], U8, align_bytes=64)

        def quantise_rows(words, codes, scales):
            planes = psum.tile([P, PAIR, HALVES, P], F32, tag="bank")
            for r in range(PAIR):
                for u in range(HALVES):
                    nc.tensor.transpose(planes[:, r, u, :], words[:, r, u * P : (u + 1) * P], ident[:])
            grouped = stage.tile([P, PAIR_COLS, PACK], BF16, align_bytes=64)
            nc.scalar.copy(
                out=grouped[:].bitcast(F32).rearrange("p (r c) u -> p r c u", r=PAIR),
                in_=planes[:].rearrange("p r u c -> p r c u"),
            )
            nc.vector.quantize_mx(
                out=codes.bitcast(FP8X4), scales=scales, in_=grouped[:].rearrange("p c t -> p (c t)")
            )

        ctx_words = ctx_sb[:].bitcast(F32)
        proj_words = proj_sb[:].bitcast(F32)
        mlp_words = mlp_sb[:].bitcast(F32)

        pieces = []
        for g in range(BRANCHES):
            for n in range(E // PAIR_COLS):
                cols = slice(n * PAIR_COLS, (n + 1) * PAIR_COLS)
                pieces.append((proj_words[:, g, n], proj_q[:, g, cols], proj_s[:, g, cols]))
            for n in range(BLOCKS):
                cols = slice(n * PAIR_COLS, (n + 1) * PAIR_COLS)
                pieces.append((ctx_words[:, g, n * PAIR : (n + 1) * PAIR], ctx_q[:, g, cols], ctx_s[:, g, cols]))
        for n in range(E // PAIR_COLS):
            cols = slice(n * PAIR_COLS, (n + 1) * PAIR_COLS)
            for g in range(BRANCHES):
                words = mlp_words[:, n * PAIR : (n + 1) * PAIR, g * PASS_WORDS : (g + 1) * PASS_WORDS]
                pieces.append((words, mlp_q[:, g, cols], mlp_s[:, g, cols]))

        proj_bias = [bias[:].rearrange("p u e -> p (u e)") for bias in proj_bias_bf]
        mlp_bias = keep.tile([P, E], F32)

        def spread_mlp_bias():
            bias_bank = psum.tile([P, E], F32, tag="bank")
            nc.tensor.matmul(out=bias_bank[:], lhsT=ones[:, :P], rhs=bias_row[:], start=True, stop=True)
            nc.scalar.copy(out=mlp_bias[:], in_=bias_bank[:])

        def project(g, i):
            toks = slice(i * P, (i + 1) * P)
            proj = psum.tile([P, CHUNKS, P], F32, tag="bank")
            for t in range(CHUNKS):
                feats = slice(t * P, (t + 1) * P)
                nc.tensor.matmul_mx(
                    out=proj[:, t, :],
                    lhsT=proj_q[:, g, feats].bitcast(FP8X4),
                    lhsT_scale=proj_s[:, g, feats],
                    rhs=ctx_q[:, g, toks].bitcast(FP8X4),
                    rhs_scale=ctx_s[:, g, toks],
                    start=True,
                    stop=True,
                )
            return proj

        def stage_one(g, b):
            first, second = project(g, b * PAIR), project(g, b * PAIR + 1)
            grouped = stage.tile([P, PAIR, P, PACK], BF16, align_bytes=64, name="grouped_combined")
            chunks = stage.tile([P, CHUNKS, P], BF16)
            for t in range(CHUNKS):
                nc.scalar.activation(
                    out=chunks[:, t, :], in_=first[:, t, :], func=IDENTITY, bias=proj_bias[g][:, t : t + 1]
                )
            nc.vector.tensor_tensor(
                out=grouped[:, 1],
                in0=second[:].rearrange("p t w -> p w t"),
                in1=proj_bias[g].unsqueeze(1).to_broadcast([P, P, CHUNKS]),
                op=ADD,
            )
            nc.vector.tensor_copy(
                out=grouped[:, 0].rearrange("p (c i) t -> p c t i", i=4),
                in_=chunks[:].rearrange("p t (c i) -> p c t i", i=4),
            )
            return grouped

        def quantise_combined(g, b, grouped):
            tokens = slice(b * BLOCK, (b + 1) * BLOCK)
            nc.vector.quantize_mx(
                out=comb_q[:, g, tokens].bitcast(FP8X4),
                scales=comb_s[:, g, tokens],
                in_=grouped[:].rearrange("p s w t -> p (s w t)"),
            )

        def stage_two(i):
            toks = slice(i * P, (i + 1) * P)
            acc = psum.tile([P, E], F32, tag="bank")
            for g in range(BRANCHES):
                nc.tensor.matmul_mx(
                    out=acc[:],
                    lhsT=comb_q[:, g, toks].bitcast(FP8X4),
                    lhsT_scale=comb_s[:, g, toks],
                    rhs=mlp_q[:, g, :].bitcast(FP8X4),
                    rhs_scale=mlp_s[:, g, :],
                    start=(g == 0),
                    stop=(g == BRANCHES - 1),
                )
            biased = results.tile([P, E], F32)
            nc.vector.tensor_tensor(out=biased[:], in0=acc[:], in1=mlp_bias[:], op=ADD)
            hidden = results.tile([P, E], F32)
            nc.scalar.activation(out=hidden[:], in_=biased[:], func=RELU)
            nc.sync.dma_start(out=out_rows[:, i, :], in_=hidden[:])

        for piece in pieces[:AHEAD]:
            quantise_rows(piece[0], piece[1], piece[2])
        step = 0
        for g in range(BRANCHES):
            for b in range(BLOCKS):
                grouped = stage_one(g, b)
                done = AHEAD + step * PER_STEP
                for piece in pieces[done : done + PER_STEP]:
                    quantise_rows(piece[0], piece[1], piece[2])
                quantise_combined(g, b, grouped)
                step += 1
        spread_mlp_bias()
        for i in range(TOKEN_TILES):
            stage_two(i)
